import numpy as np
import ml_dtypes


def mxq(x, axis, fmt="e4m3"):
    dtype, down = {"e4m3": (ml_dtypes.float8_e4m3fn, 7), "e5m2": (ml_dtypes.float8_e5m2, 14)}[fmt]
    v = np.moveaxis(np.asarray(x, np.float32).astype(ml_dtypes.bfloat16).astype(np.float64), axis, -1)
    blocks = v.reshape(v.shape[:-1] + (-1, 32))
    amax = np.abs(blocks).max(-1, keepdims=True)
    byte = np.maximum(np.where(amax > 0, np.frexp(amax)[1] - 1 + 127, 0) - down, 1)
    scale = np.exp2(byte - 127.0)
    codes = (blocks / scale).astype(np.float32).astype(dtype).astype(np.float64)
    return np.moveaxis((codes * scale).reshape(v.shape), -1, axis)


WIDE = False


def mx_kscale(k):
    if not WIDE:
        return np.ones(k)
    levels = np.array([10, -10, 5, -5, 0])
    a = np.random.permutation(np.resize(levels, k // 512 * 4)).reshape(k // 512, 4)
    idx = np.arange(k)
    return np.exp2(a[idx // 512, idx % 128 // 32])


BF16 = ml_dtypes.bfloat16


def bf(x):
    return np.asarray(x, np.float32).astype(BF16)


def f64(x):
    return np.asarray(x).astype(np.float64)


B, T, E, V, H, C = 2, 2048, 512, 2048, 4, 512
KD = E // H
ROPE_BASE = 10000.0


def rotate_every_two(u):
    u1 = u[..., ::2]
    u2 = u[..., 1::2]
    return np.stack((-u2, u1), axis=-1).reshape(u.shape)


def theta_shift(u, sin, cos):
    return u * cos + rotate_every_two(u) * sin


def setup_inputs():
    s = mx_kscale(E)
    angle = np.arange(T)[:, None] * (1.0 / ROPE_BASE ** (np.repeat(np.arange(KD // 2), 2) * 2.0 / KD))
    return {"x": bf(np.random.standard_normal((B, T, E)) * s),
            "sin": bf(np.sin(angle)), "cos": bf(np.cos(angle)),
            "Wq": bf(np.random.standard_normal((E, E)) * 0.5 / np.sqrt(E) / s[:, None]),
            "Wk": bf(np.random.standard_normal((E, E)) * 2.0 / np.sqrt(E) / s[:, None])}


def reference(x, sin, cos, Wq, Wk):
    xq = mxq(f64(x), 2, "e4m3")
    q = (xq @ mxq(f64(Wq), 0, "e4m3")).reshape(B, T, H, KD).transpose(0, 2, 1, 3)
    k = ((xq @ mxq(f64(Wk), 0, "e4m3")) * KD ** -0.5).reshape(B, T, H, KD).transpose(0, 2, 1, 3)
    return theta_shift(q, f64(sin), f64(cos)), theta_shift(k, f64(sin), f64(cos))

@@ -1,0 +1,154 @@
+from contextlib import ExitStack
+
+import concourse.mybir as mybir
+from concourse.masks import make_identity
+
+F32 = mybir.dt.float32
+BF16 = mybir.dt.bfloat16
+U32 = mybir.dt.uint32
+U8 = mybir.dt.uint8
+FP8X4 = mybir.dt.float8_e4m3fn_x4
+MULT = mybir.AluOpType.mult
+ADD = mybir.AluOpType.add
+
+P = 128
+PACK = 4
+BATCH, SEQ, WIDTH = 2, 2048, 512
+HEADS, HEAD_DIM = 4, 128
+ROWS = 4
+GROUP = P * ROWS
+GROUPS_PER_SEQ = SEQ // GROUP
+WORDS = WIDTH // 2
+
+FLOPS = 2 * BATCH * SEQ * WIDTH * (2 * WIDTH)
+
+
+def quantise_weight(nc, pools, w):
+    w_rows = pools["weights"].tile([P, PACK, WIDTH], BF16)
+    nc.sync.dma_start(
+        out=w_rows[:].rearrange("p (u e) c -> p u (e c)", u=2),
+        in_=w.rearrange("(u p e) c -> p u (e c)", u=2, p=P),
+    )
+    w_grouped = pools["weights"].tile([P, 2, WIDTH, PACK], BF16, align_bytes=64)
+    nc.vector.tensor_copy(out=w_grouped[:, 0], in_=w_rows[:].rearrange("p t c -> p c t"))
+    turned = w_grouped[:, 1].rearrange("p (i e) t -> p i e t", e=2)
+    pairs = w_rows[:].rearrange("p t (i e) -> p i e t", e=2)
+    nc.scalar.mul(out=turned[:, :, 0, :], in_=pairs[:, :, 1, :], mul=-1.0)
+    nc.scalar.copy(out=turned[:, :, 1, :], in_=pairs[:, :, 0, :])
+    w_codes = pools["weights"].tile([P, 2, WIDTH], U32, align_bytes=64)
+    w_scales = pools["weights"].tile([P, 2, WIDTH], U8, align_bytes=64)
+    nc.vector.quantize_mx(
+        out=w_codes[:].rearrange("p v c -> p (v c)").bitcast(FP8X4),
+        scales=w_scales[:].rearrange("p v c -> p (v c)"),
+        in_=w_grouped[:].rearrange("p v c t -> p (v c t)"),
+    )
+    return w_codes, w_scales
+
+
+def quantise_positions(nc, pools, identity, x_rows):
+    x_grouped = pools["x_mx"].tile([P, GROUP, PACK], BF16, align_bytes=64)
+    grouped_words = x_grouped[:].bitcast(F32)
+    for half in range(ROWS // 2):
+        x_t = pools["psum_t"].tile([P, 2, 2, P], F32)
+        for r in range(2):
+            words = x_rows[:, 2 * half + r, :].bitcast(F32)
+            for u in range(2):
+                nc.tensor.transpose(x_t[:, r, u, :], words[:, u * P : (u + 1) * P], identity[:])
+        nc.scalar.copy(
+            out=grouped_words[:, 2 * half * P : 2 * (half + 1) * P, :].rearrange(
+                "p (r m) u -> p r m u", r=2
+            ),
+            in_=x_t[:].rearrange("p r u m -> p r m u"),
+        )
+    x_codes = pools["x_mx"].tile([P, GROUP], U32, align_bytes=64)
+    x_scales = pools["x_mx"].tile([P, GROUP], U8, align_bytes=64)
+    nc.vector.quantize_mx(
+        out=x_codes[:].bitcast(FP8X4),
+        scales=x_scales[:],
+        in_=x_grouped[:].rearrange("p m t -> p (m t)"),
+    )
+    return x_codes, x_scales
+
+
+def tile_multiscaleretention_pa_t_kernel(tc, x, sin, cos, Wq, Wk, out_0, out_1):
+    nc = tc.nc
+    groups = [(b, g) for b in range(BATCH) for g in range(GROUPS_PER_SEQ)]
+    with ExitStack() as stack:
+        pools = {
+            "const": stack.enter_context(tc.tile_pool(name="const", bufs=1)),
+            "weights": stack.enter_context(tc.tile_pool(name="weights", bufs=2)),
+            "x_rows": stack.enter_context(tc.tile_pool(name="x_rows", bufs=len(groups))),
+            "x_mx": stack.enter_context(tc.tile_pool(name="x_mx", bufs=2)),
+            "result": stack.enter_context(tc.tile_pool(name="result", bufs=3)),
+            "psum_t": stack.enter_context(tc.psum_pool(name="psum_t", bufs=2)),
+            "psum_mx": stack.enter_context(tc.psum_pool(name="psum_mx", bufs=3)),
+        }
+        identity = pools["const"].tile([P, P], F32)
+        make_identity(nc, identity[:])
+
+        def by_group(rows):
+            return rows.rearrange("(g p r) c -> g p r c", p=P, r=ROWS)
+
+        weights = {"q": quantise_weight(nc, pools, Wq)}
+        all_x_rows = []
+        for b, g in groups[:1]:
+            x_rows = pools["x_rows"].tile([P, ROWS, WIDTH], BF16)
+            nc.sync.dma_start(out=x_rows[:], in_=by_group(x[b])[g])
+            all_x_rows.append(x_rows)
+        cos_q = pools["const"].tile([P, GROUPS_PER_SEQ, ROWS, HEAD_DIM], BF16)
+        sin_q = pools["const"].tile([P, GROUPS_PER_SEQ, ROWS, HEAD_DIM], BF16)
+        nc.sync.dma_start(out=cos_q[:], in_=cos.rearrange("(g p r) c -> p g r c", p=P, r=ROWS))
+        nc.sync.dma_start(out=sin_q[:], in_=sin.rearrange("(g p r) c -> p g r c", p=P, r=ROWS))
+        weights["k"] = quantise_weight(nc, pools, Wk)
+        for b, g in groups[1:]:
+            x_rows = pools["x_rows"].tile([P, ROWS, WIDTH], BF16)
+            nc.sync.dma_start(out=x_rows[:], in_=by_group(x[b])[g])
+            all_x_rows.append(x_rows)
+
+        cos_k = pools["const"].tile([P, GROUPS_PER_SEQ, ROWS, HEAD_DIM], F32)
+        sin_k = pools["const"].tile([P, GROUPS_PER_SEQ, ROWS, HEAD_DIM], F32)
+        for g in range(GROUPS_PER_SEQ):
+            nc.scalar.mul(out=cos_k[:, g], in_=cos_q[:, g], mul=HEAD_DIM**-0.5)
+            nc.scalar.mul(out=sin_k[:, g], in_=sin_q[:, g], mul=HEAD_DIM**-0.5)
+        tables = {"q": (cos_q, sin_q), "k": (cos_k, sin_k)}
+        outputs = {"q": out_0, "k": out_1}
+
+        x_mx = quantise_positions(nc, pools, identity, all_x_rows[0])
+        for n, (b, g) in enumerate(groups):
+            x_codes, x_scales = x_mx
+            if n + 1 < len(groups):
+                x_mx = quantise_positions(nc, pools, identity, all_x_rows[n + 1])
+            for which in ("q", "k"):
+                w_codes, w_scales = weights[which]
+                cos_t, sin_t = tables[which]
+                by_cos = pools["result"].tile([P, HEADS, ROWS, HEAD_DIM], F32)
+                by_sin = pools["result"].tile([P, HEADS, ROWS, HEAD_DIM], F32)
+                for r in range(ROWS):
+                    positions = slice(r * P, (r + 1) * P)
+                    for v, table, product in ((0, cos_t, by_cos), (1, sin_t, by_sin)):
+                        projected = pools["psum_mx"].tile([P, WIDTH], F32, tag="projected%d" % v)
+                        nc.tensor.matmul_mx(
+                            out=projected[:],
+                            lhsT=x_codes[:, positions].bitcast(FP8X4),
+                            lhsT_scale=x_scales[:, positions],
+                            rhs=w_codes[:, v, :].bitcast(FP8X4),
+                            rhs_scale=w_scales[:, v, :],
+                            start=True,
+                            stop=True,
+                        )
+                        nc.vector.tensor_tensor(
+                            out=product[:, :, r, :],
+                            in0=projected[:].rearrange("p (h c) -> p h c", h=HEADS),
+                            in1=table[:, g, r, :].unsqueeze(1).to_broadcast([P, HEADS, HEAD_DIM]),
+                            op=MULT,
+                        )
+                nc.gpsimd.tensor_tensor(
+                    out=by_cos[:].rearrange("p h r c -> p (h r c)"),
+                    in0=by_cos[:].rearrange("p h r c -> p (h r c)"),
+                    in1=by_sin[:].rearrange("p h r c -> p (h r c)"),
+                    op=ADD,
+                )
+                nc.sync.dma_start(
+                    out=outputs[which][b].rearrange("h (g p r) c -> g p h (r c)", p=P, r=ROWS)[g],
+                    in_=by_cos[:].rearrange("p h r c -> p h (r c)"),
+                )

@@ -18,19 +18,22 @@ HEADS, HEAD_DIM = 4, 128
 ROWS = 4
 GROUP = P * ROWS
 GROUPS_PER_SEQ = SEQ // GROUP
-WORDS = WIDTH // 2
 
 FLOPS = 2 * BATCH * SEQ * WIDTH * (2 * WIDTH)
 
 
-def quantise_weight(nc, pools, w):
+def load_weight(nc, pools, w):
     w_rows = pools["weights"].tile([P, PACK, WIDTH], BF16)
     nc.sync.dma_start(
         out=w_rows[:].rearrange("p (u e) c -> p u (e c)", u=2),
         in_=w.rearrange("(u p e) c -> p u (e c)", u=2, p=P),
     )
+    return w_rows
+
+
+def quantise_weight(nc, pools, w_rows, plain_copy):
     w_grouped = pools["weights"].tile([P, 2, WIDTH, PACK], BF16, align_bytes=64)
-    nc.vector.tensor_copy(out=w_grouped[:, 0], in_=w_rows[:].rearrange("p t c -> p c t"))
+    plain_copy(out=w_grouped[:, 0], in_=w_rows[:].rearrange("p t c -> p c t"))
     turned = w_grouped[:, 1].rearrange("p (i e) t -> p i e t", e=2)
     pairs = w_rows[:].rearrange("p t (i e) -> p i e t", e=2)
     nc.scalar.mul(out=turned[:, :, 0, :], in_=pairs[:, :, 1, :], mul=-1.0)
@@ -79,76 +82,84 @@ def tile_multiscaleretention_pa_t_kernel(tc, x, sin, cos, Wq, Wk, out_0, out_1):
             "weights": stack.enter_context(tc.tile_pool(name="weights", bufs=2)),
             "x_rows": stack.enter_context(tc.tile_pool(name="x_rows", bufs=len(groups))),
             "x_mx": stack.enter_context(tc.tile_pool(name="x_mx", bufs=2)),
-            "result": stack.enter_context(tc.tile_pool(name="result", bufs=3)),
+            "result": stack.enter_context(tc.tile_pool(name="result", bufs=4)),
             "psum_t": stack.enter_context(tc.psum_pool(name="psum_t", bufs=2)),
             "psum_mx": stack.enter_context(tc.psum_pool(name="psum_mx", bufs=3)),
         }
         identity = pools["const"].tile([P, P], F32)
         make_identity(nc, identity[:])
 
-        def by_group(rows):
-            return rows.rearrange("(g p r) c -> g p r c", p=P, r=ROWS)
-
-        weights = {"q": quantise_weight(nc, pools, Wq)}
-        all_x_rows = []
-        for b, g in groups[:1]:
+        def load_positions(b, g):
             x_rows = pools["x_rows"].tile([P, ROWS, WIDTH], BF16)
-            nc.sync.dma_start(out=x_rows[:], in_=by_group(x[b])[g])
-            all_x_rows.append(x_rows)
-        cos_q = pools["const"].tile([P, GROUPS_PER_SEQ, ROWS, HEAD_DIM], BF16)
-        sin_q = pools["const"].tile([P, GROUPS_PER_SEQ, ROWS, HEAD_DIM], BF16)
-        nc.sync.dma_start(out=cos_q[:], in_=cos.rearrange("(g p r) c -> p g r c", p=P, r=ROWS))
-        nc.sync.dma_start(out=sin_q[:], in_=sin.rearrange("(g p r) c -> p g r c", p=P, r=ROWS))
-        weights["k"] = quantise_weight(nc, pools, Wk)
+            nc.sync.dma_start(
+                out=x_rows[:], in_=x[b].rearrange("(g p r) c -> g p r c", p=P, r=ROWS)[g]
+            )
+            return x_rows
+
+        def load_table(table, name):
+            rows = pools["const"].tile([P, GROUPS_PER_SEQ, ROWS, HEAD_DIM], BF16, name=name)
+            nc.sync.dma_start(out=rows[:], in_=table.rearrange("(g p r) c -> p g r c", p=P, r=ROWS))
+            return rows
+
+        w_rows = {"q": load_weight(nc, pools, Wq)}
+        x_groups = [load_positions(*groups[0])]
+        tables = (load_table(cos, "cos_rows"), load_table(sin, "sin_rows"))
+        w_rows["k"] = load_weight(nc, pools, Wk)
         for b, g in groups[1:]:
-            x_rows = pools["x_rows"].tile([P, ROWS, WIDTH], BF16)
-            nc.sync.dma_start(out=x_rows[:], in_=by_group(x[b])[g])
-            all_x_rows.append(x_rows)
+            x_groups.append(load_positions(b, g))
 
-        cos_k = pools["const"].tile([P, GROUPS_PER_SEQ, ROWS, HEAD_DIM], F32)
-        sin_k = pools["const"].tile([P, GROUPS_PER_SEQ, ROWS, HEAD_DIM], F32)
-        for g in range(GROUPS_PER_SEQ):
-            nc.scalar.mul(out=cos_k[:, g], in_=cos_q[:, g], mul=HEAD_DIM**-0.5)
-            nc.scalar.mul(out=sin_k[:, g], in_=sin_q[:, g], mul=HEAD_DIM**-0.5)
-        tables = {"q": (cos_q, sin_q), "k": (cos_k, sin_k)}
+        factor = {"q": 1.0, "k": HEAD_DIM**-0.5}
         outputs = {"q": out_0, "k": out_1}
+        weights = {}
 
-        x_mx = quantise_positions(nc, pools, identity, all_x_rows[0])
+        def project_and_rotate(which, b, g, x_codes, x_scales, adder, rows_at_once):
+            w_codes, w_scales = weights[which]
+            out_rows = outputs[which][b].rearrange("h (g p r) c -> g p h r c", p=P, r=ROWS)[g]
+            products = [
+                pools["result"].tile([P, HEADS, ROWS, HEAD_DIM], F32, name="by_cos"),
+                pools["result"].tile([P, HEADS, ROWS, HEAD_DIM], F32, name="by_sin"),
+            ]
+            for r in range(ROWS):
+                positions = slice(r * P, (r + 1) * P)
+                for v in range(2):
+                    projected = pools["psum_mx"].tile([P, WIDTH], F32, tag="projected%d" % v)
+                    nc.tensor.matmul_mx(
+                        out=projected[:],
+                        lhsT=x_codes[:, positions].bitcast(FP8X4),
+                        lhsT_scale=x_scales[:, positions],
+                        rhs=w_codes[:, v, :].bitcast(FP8X4),
+                        rhs_scale=w_scales[:, v, :],
+                        start=True,
+                        stop=True,
+                    )
+                    nc.vector.scalar_tensor_tensor(
+                        out=products[v][:, :, r, :],
+                        in0=projected[:].rearrange("p (h c) -> p h c", h=HEADS),
+                        scalar=factor[which],
+                        in1=tables[v][:, g, r, :].unsqueeze(1).to_broadcast([P, HEADS, HEAD_DIM]),
+                        op0=MULT,
+                        op1=MULT,
+                    )
+                if (r + 1) % rows_at_once == 0:
+                    done = slice(r + 1 - rows_at_once, r + 1)
+                    adder.tensor_tensor(
+                        out=products[0][:, :, done, :],
+                        in0=products[0][:, :, done, :],
+                        in1=products[1][:, :, done, :],
+                        op=ADD,
+                    )
+                    nc.sync.dma_start(out=out_rows[:, :, done, :], in_=products[0][:, :, done, :])
+
+        weights["q"] = quantise_weight(nc, pools, w_rows["q"], nc.vector.tensor_copy)
+        x_mx = quantise_positions(nc, pools, identity, x_groups[0])
         for n, (b, g) in enumerate(groups):
-            x_codes, x_scales = x_mx
-            if n + 1 < len(groups):
-                x_mx = quantise_positions(nc, pools, identity, all_x_rows[n + 1])
-            for which in ("q", "k"):
-                w_codes, w_scales = weights[which]
-                cos_t, sin_t = tables[which]
-                by_cos = pools["result"].tile([P, HEADS, ROWS, HEAD_DIM], F32)
-                by_sin = pools["result"].tile([P, HEADS, ROWS, HEAD_DIM], F32)
-                for r in range(ROWS):
-                    positions = slice(r * P, (r + 1) * P)
-                    for v, table, product in ((0, cos_t, by_cos), (1, sin_t, by_sin)):
-                        projected = pools["psum_mx"].tile([P, WIDTH], F32, tag="projected%d" % v)
-                        nc.tensor.matmul_mx(
-                            out=projected[:],
-                            lhsT=x_codes[:, positions].bitcast(FP8X4),
-                            lhsT_scale=x_scales[:, positions],
-                            rhs=w_codes[:, v, :].bitcast(FP8X4),
-                            rhs_scale=w_scales[:, v, :],
-                            start=True,
-                            stop=True,
-                        )
-                        nc.vector.tensor_tensor(
-                            out=product[:, :, r, :],
-                            in0=projected[:].rearrange("p (h c) -> p h c", h=HEADS),
-                            in1=table[:, g, r, :].unsqueeze(1).to_broadcast([P, HEADS, HEAD_DIM]),
-                            op=MULT,
-                        )
-                nc.gpsimd.tensor_tensor(
-                    out=by_cos[:].rearrange("p h r c -> p (h r c)"),
-                    in0=by_cos[:].rearrange("p h r c -> p (h r c)"),
-                    in1=by_sin[:].rearrange("p h r c -> p (h r c)"),
-                    op=ADD,
-                )
-                nc.sync.dma_start(
-                    out=outputs[which][b].rearrange("h (g p r) c -> g p h (r c)", p=P, r=ROWS)[g],
-                    in_=by_cos[:].rearrange("p h r c -> p h (r c)"),
-                )
+            last = n + 1 == len(groups)
+            project_and_rotate("q", b, g, x_mx[0], x_mx[1], nc.gpsimd, ROWS)
+            if n == 0:
+                weights["k"] = quantise_weight(nc, pools, w_rows["k"], nc.scalar.copy)
+            if not last:
+                next_x_mx = quantise_positions(nc, pools, identity, x_groups[n + 1])
+                project_and_rotate("k", b, g, x_mx[0], x_mx[1], nc.gpsimd, ROWS)
+                x_mx = next_x_mx
+            else:
+                project_and_rotate("k", b, g, x_mx[0], x_mx[1], nc.vector, 1)

@@ -77,6 +77,7 @@ def tile_multiscaleretention_pa_t_kernel(tc, x, sin, cos, Wq, Wk, out_0, out_1):
     nc = tc.nc
     groups = [(b, g) for b in range(BATCH) for g in range(GROUPS_PER_SEQ)]
     with ExitStack() as stack:
+        stack.enter_context(tc.manual_schedule())
         pools = {
             "const": stack.enter_context(tc.tile_pool(name="const", bufs=1)),
             "weights": stack.enter_context(tc.tile_pool(name="weights", bufs=2)),
@@ -140,15 +141,15 @@ def tile_multiscaleretention_pa_t_kernel(tc, x, sin, cos, Wq, Wk, out_0, out_1):
                         op0=MULT,
                         op1=MULT,
                     )
-                if (r + 1) % rows_at_once == 0:
-                    done = slice(r + 1 - rows_at_once, r + 1)
-                    adder.tensor_tensor(
-                        out=products[0][:, :, done, :],
-                        in0=products[0][:, :, done, :],
-                        in1=products[1][:, :, done, :],
-                        op=ADD,
-                    )
-                    nc.sync.dma_start(out=out_rows[:, :, done, :], in_=products[0][:, :, done, :])
+            for first in range(0, ROWS, rows_at_once):
+                done = slice(first, first + rows_at_once)
+                adder.tensor_tensor(
+                    out=products[0][:, :, done, :],
+                    in0=products[0][:, :, done, :],
+                    in1=products[1][:, :, done, :],
+                    op=ADD,
+                )
+                nc.sync.dma_start(out=out_rows[:, :, done, :], in_=products[0][:, :, done, :])
 
         weights["q"] = quantise_weight(nc, pools, w_rows["q"], nc.vector.tensor_copy)
         x_mx = quantise_positions(nc, pools, identity, x_groups[0])

from contextlib import ExitStack

import concourse.mybir as mybir
from concourse.masks import make_identity

F32 = mybir.dt.float32
BF16 = mybir.dt.bfloat16
U32 = mybir.dt.uint32
U8 = mybir.dt.uint8
FP8X4 = mybir.dt.float8_e4m3fn_x4
MULT = mybir.AluOpType.mult
ADD = mybir.AluOpType.add

P = 128
PACK = 4
BATCH, SEQ, WIDTH = 2, 2048, 512
HEADS, HEAD_DIM = 4, 128
ROWS = 4
GROUP = P * ROWS
GROUPS_PER_SEQ = SEQ // GROUP

FLOPS = 2 * BATCH * SEQ * WIDTH * (2 * WIDTH)


def load_weight(nc, pools, w):
    w_rows = pools["weights"].tile([P, PACK, WIDTH], BF16)
    nc.sync.dma_start(
        out=w_rows[:].rearrange("p (u e) c -> p u (e c)", u=2),
        in_=w.rearrange("(u p e) c -> p u (e c)", u=2, p=P),
    )
    return w_rows


def quantise_weight(nc, pools, w_rows, plain_copy):
    w_grouped = pools["weights"].tile([P, 2, WIDTH, PACK], BF16, align_bytes=64)
    plain_copy(out=w_grouped[:, 0], in_=w_rows[:].rearrange("p t c -> p c t"))
    turned = w_grouped[:, 1].rearrange("p (i e) t -> p i e t", e=2)
    pairs = w_rows[:].rearrange("p t (i e) -> p i e t", e=2)
    nc.scalar.mul(out=turned[:, :, 0, :], in_=pairs[:, :, 1, :], mul=-1.0)
    nc.scalar.copy(out=turned[:, :, 1, :], in_=pairs[:, :, 0, :])
    w_codes = pools["weights"].tile([P, 2, WIDTH], U32, align_bytes=64)
    w_scales = pools["weights"].tile([P, 2, WIDTH], U8, align_bytes=64)
    nc.vector.quantize_mx(
        out=w_codes[:].rearrange("p v c -> p (v c)").bitcast(FP8X4),
        scales=w_scales[:].rearrange("p v c -> p (v c)"),
        in_=w_grouped[:].rearrange("p v c t -> p (v c t)"),
    )
    return w_codes, w_scales


def quantise_positions(nc, pools, identity, x_rows):
    x_grouped = pools["x_mx"].tile([P, GROUP, PACK], BF16, align_bytes=64)
    grouped_words = x_grouped[:].bitcast(F32)
    for half in range(ROWS // 2):
        x_t = pools["psum_t"].tile([P, 2, 2, P], F32)
        for r in range(2):
            words = x_rows[:, 2 * half + r, :].bitcast(F32)
            for u in range(2):
                nc.tensor.transpose(x_t[:, r, u, :], words[:, u * P : (u + 1) * P], identity[:])
        nc.scalar.copy(
            out=grouped_words[:, 2 * half * P : 2 * (half + 1) * P, :].rearrange(
                "p (r m) u -> p r m u", r=2
            ),
            in_=x_t[:].rearrange("p r u m -> p r m u"),
        )
    x_codes = pools["x_mx"].tile([P, GROUP], U32, align_bytes=64)
    x_scales = pools["x_mx"].tile([P, GROUP], U8, align_bytes=64)
    nc.vector.quantize_mx(
        out=x_codes[:].bitcast(FP8X4),
        scales=x_scales[:],
        in_=x_grouped[:].rearrange("p m t -> p (m t)"),
    )
    return x_codes, x_scales


def tile_multiscaleretention_pa_t_kernel(tc, x, sin, cos, Wq, Wk, out_0, out_1):
    nc = tc.nc
    groups = [(b, g) for b in range(BATCH) for g in range(GROUPS_PER_SEQ)]
    with ExitStack() as stack:
        stack.enter_context(tc.manual_schedule())
        pools = {
            "const": stack.enter_context(tc.tile_pool(name="const", bufs=1)),
            "weights": stack.enter_context(tc.tile_pool(name="weights", bufs=2)),
            "x_rows": stack.enter_context(tc.tile_pool(name="x_rows", bufs=len(groups))),
            "x_mx": stack.enter_context(tc.tile_pool(name="x_mx", bufs=2)),
            "result": stack.enter_context(tc.tile_pool(name="result", bufs=4)),
            "psum_t": stack.enter_context(tc.psum_pool(name="psum_t", bufs=2)),
            "psum_mx": stack.enter_context(tc.psum_pool(name="psum_mx", bufs=3)),
        }
        identity = pools["const"].tile([P, P], F32)
        make_identity(nc, identity[:])

        def load_positions(b, g):
            x_rows = pools["x_rows"].tile([P, ROWS, WIDTH], BF16)
            nc.sync.dma_start(
                out=x_rows[:], in_=x[b].rearrange("(g p r) c -> g p r c", p=P, r=ROWS)[g]
            )
            return x_rows

        def load_table(table, name):
            rows = pools["const"].tile([P, GROUPS_PER_SEQ, ROWS, HEAD_DIM], BF16, name=name)
            nc.sync.dma_start(out=rows[:], in_=table.rearrange("(g p r) c -> p g r c", p=P, r=ROWS))
            return rows

        w_rows = {"q": load_weight(nc, pools, Wq)}
        x_groups = [load_positions(*groups[0])]
        tables = (load_table(cos, "cos_rows"), load_table(sin, "sin_rows"))
        w_rows["k"] = load_weight(nc, pools, Wk)
        for b, g in groups[1:]:
            x_groups.append(load_positions(b, g))

        factor = {"q": 1.0, "k": HEAD_DIM**-0.5}
        outputs = {"q": out_0, "k": out_1}
        weights = {}

        def project_and_rotate(which, b, g, x_codes, x_scales, adder, rows_at_once):
            w_codes, w_scales = weights[which]
            out_rows = outputs[which][b].rearrange("h (g p r) c -> g p h r c", p=P, r=ROWS)[g]
            products = [
                pools["result"].tile([P, HEADS, ROWS, HEAD_DIM], F32, name="by_cos"),
                pools["result"].tile([P, HEADS, ROWS, HEAD_DIM], F32, name="by_sin"),
            ]
            for r in range(ROWS):
                positions = slice(r * P, (r + 1) * P)
                for v in range(2):
                    projected = pools["psum_mx"].tile([P, WIDTH], F32, tag="projected%d" % v)
                    nc.tensor.matmul_mx(
                        out=projected[:],
                        lhsT=x_codes[:, positions].bitcast(FP8X4),
                        lhsT_scale=x_scales[:, positions],
                        rhs=w_codes[:, v, :].bitcast(FP8X4),
                        rhs_scale=w_scales[:, v, :],
                        start=True,
                        stop=True,
                    )
                    nc.vector.scalar_tensor_tensor(
                        out=products[v][:, :, r, :],
                        in0=projected[:].rearrange("p (h c) -> p h c", h=HEADS),
                        scalar=factor[which],
                        in1=tables[v][:, g, r, :].unsqueeze(1).to_broadcast([P, HEADS, HEAD_DIM]),
                        op0=MULT,
                        op1=MULT,
                    )
            for first in range(0, ROWS, rows_at_once):
                done = slice(first, first + rows_at_once)
                adder.tensor_tensor(
                    out=products[0][:, :, done, :],
                    in0=products[0][:, :, done, :],
                    in1=products[1][:, :, done, :],
                    op=ADD,
                )
                nc.sync.dma_start(out=out_rows[:, :, done, :], in_=products[0][:, :, done, :])

        weights["q"] = quantise_weight(nc, pools, w_rows["q"], nc.vector.tensor_copy)
        x_mx = quantise_positions(nc, pools, identity, x_groups[0])
        for n, (b, g) in enumerate(groups):
            last = n + 1 == len(groups)
            project_and_rotate("q", b, g, x_mx[0], x_mx[1], nc.gpsimd, ROWS)
            if n == 0:
                weights["k"] = quantise_weight(nc, pools, w_rows["k"], nc.scalar.copy)
            if not last:
                next_x_mx = quantise_positions(nc, pools, identity, x_groups[n + 1])
                project_and_rotate("k", b, g, x_mx[0], x_mx[1], nc.gpsimd, ROWS)
                x_mx = next_x_mx
            else:
                project_and_rotate("k", b, g, x_mx[0], x_mx[1], nc.vector, 1)
